import numpy as np
import ml_dtypes


def mxq(x, axis, fmt="e4m3"):
    dtype, down = {"e4m3": (ml_dtypes.float8_e4m3fn, 7), "e5m2": (ml_dtypes.float8_e5m2, 14)}[fmt]
    v = np.moveaxis(np.asarray(x, np.float32).astype(ml_dtypes.bfloat16).astype(np.float64), axis, -1)
    blocks = v.reshape(v.shape[:-1] + (-1, 32))
    amax = np.abs(blocks).max(-1, keepdims=True)
    byte = np.maximum(np.where(amax > 0, np.frexp(amax)[1] - 1 + 127, 0) - down, 1)
    scale = np.exp2(byte - 127.0)
    codes = (blocks / scale).astype(np.float32).astype(dtype).astype(np.float64)
    return np.moveaxis((codes * scale).reshape(v.shape), -1, axis)


WIDE = False


def mx_kscale(k):
    if not WIDE:
        return np.ones(k)
    levels = np.array([30, -30])
    if k % 512:
        return np.exp2(np.random.permutation(np.resize(levels, k // 32))).repeat(32)
    a = np.empty((k // 512, 16))
    for p in range(k // 512):
        a[p, :8] = np.random.permutation(np.resize(levels, 8))
        for g in range(8):
            far = levels[np.abs(levels - a[p, g]) >= 10]
            a[p, g + 8] = far[np.random.randint(len(far))]
    return np.exp2(a.ravel()).repeat(32)


BF16 = ml_dtypes.bfloat16


def bf(x):
    return np.asarray(x, np.float32).astype(BF16)


def f64(x):
    return np.asarray(x).astype(np.float64)


B, T, D, H = 8, 128, 1024, 1024


def sigmoid(v):
    return 1.0 / (1.0 + np.exp(-v))


def setup_inputs():
    s = mx_kscale(D)
    return {"x": bf(np.random.standard_normal((B, T, D)) * s),
            "Wq": bf(np.random.standard_normal((H, D)) * 1.0 / np.sqrt(D) / s),
            "bq": bf(np.random.standard_normal(H) * 0.5),
            "Wk": bf(np.random.standard_normal((H, D)) * 0.6 / np.sqrt(D) / s),
            "bk": bf(np.random.standard_normal(H) * 0.3),
            "Wv": bf(np.random.standard_normal((H, D)) * 2.0 / np.sqrt(D) / s),
            "bv": bf(np.random.standard_normal(H) * 0.5),
            "wbias": bf(np.random.uniform(0.0, 1.0, H))}


def reference(x, Wq, bq, Wk, bk, Wv, bv, wbias):
    xq = mxq(f64(x), 2, "e5m2")
    Q = (xq @ mxq(f64(Wq), 1, "e4m3").T) + f64(bq)
    K = (xq @ mxq(f64(Wk), 1, "e4m3").T) + f64(bk)
    V = (xq @ mxq(f64(Wv), 1, "e4m3").T) + f64(bv)
    Q_sig = sigmoid(Q)
    numer = np.exp(K + f64(wbias))
    denom = numer.sum(axis=0)
    weighted = (numer * V).sum(axis=0) / denom
    Yt = Q_sig * weighted
    return Yt

@@ -1,0 +1,304 @@
+from contextlib import ExitStack
+
+import concourse.mybir as mybir
+from concourse.masks import make_identity
+
+B, T, D, H = 8, 128, 1024, 1024
+FLOPS = 3 * 2 * B * T * D * H
+
+F32 = mybir.dt.float32
+BF16 = mybir.dt.bfloat16
+U32 = mybir.dt.uint32
+U8 = mybir.dt.uint8
+E4M3 = mybir.dt.float8_e4m3fn_x4
+E5M2 = mybir.dt.float8_e5m2_x4
+ALU = mybir.AluOpType
+ACT = mybir.ActivationFunctionType
+
+P = 128
+PASSES = 2
+NCH = H // P
+HALF = 512
+LQ = 1
+POOL = False
+LNCH = 6
+PRE_X = 0
+PRE_DVE = ()
+PRE_ACT = ()
+XCOPY_DVE = ()
+
+
+def tile_aftattention_kernel(tc, x, Wq, bq, Wk, bk, Wv, bv, wbias, out):
+    nc = tc.nc
+    with ExitStack() as ctx:
+        keep = ctx.enter_context(tc.tile_pool(name="keep", bufs=1))
+        work = ctx.enter_context(tc.tile_pool(name="work", bufs=3))
+        psum = ctx.enter_context(tc.psum_pool(name="psum", bufs=8))
+        ctx.enter_context(tc.manual_schedule())
+
+        def bank(shape, dtype=F32):
+            return psum.tile(shape, dtype, name="bank", tag="bank")
+
+        weights = {"q": Wq, "k": Wk, "v": Wv}
+        raw = {}
+
+        def load(key, src):
+            raw[key] = keep.tile([P, D], BF16, name="raw_%s%d" % key)
+            nc.sync.dma_start(out=raw[key][:], in_=src)
+
+        def load_w(n, j):
+            load((n, j), weights[n][j * P : (j + 1) * P, :])
+
+        load_w("k", 0)
+        for b in range(4):
+            load(("x", b), x[b])
+        brows = keep.tile([P, P], BF16, name="brows")
+        nc.vector.memset(brows[:], 0.0)
+        for i, v in enumerate((bq, bk, bv, wbias)):
+            nc.sync.dma_start(out=brows[NCH * i : NCH * (i + 1), :], in_=v.rearrange("(c p) -> c p", p=P))
+        load_w("v", 0)
+        for b in range(4, 8):
+            load(("x", b), x[b])
+        for s in range(1, NCH + LQ):
+            if s < NCH:
+                load_w("k", s)
+                load_w("v", s)
+            if 0 <= s - LQ < NCH:
+                load_w("q", s - LQ)
+
+        ident = keep.tile([P, P], F32, name="ident")
+        make_identity(nc, ident[:])
+        ident_bf = keep.tile([P, P], BF16, name="ident_bf")
+        nc.scalar.activation(out=ident_bf[:], in_=ident[:], func=ACT.Copy)
+        bcols = keep.tile([P, 4 * NCH], F32, name="bcols")
+        bq_half = keep.tile([P, NCH], F32, name="bq_half")
+        bkw = keep.tile([P, NCH], F32, name="bkw")
+
+        def bias_setup():
+            bb = bank([P, P], BF16)
+            nc.tensor.transpose(bb[:], brows[:], ident_bf[:])
+            nc.vector.tensor_copy(out=bcols[:], in_=bb[:, : 4 * NCH])
+
+        def bias_setup2():
+            nc.vector.tensor_scalar(out=bq_half[:], in0=bcols[:, 0:NCH], scalar1=0.5, scalar2=None, op0=ALU.mult)
+            nc.vector.tensor_tensor(out=bkw[:], in0=bcols[:, NCH : 2 * NCH], in1=bcols[:, 3 * NCH :], op=ALU.add)
+
+        x_codes = keep.tile([P, PASSES, B * T], U32, name="x_codes", align_bytes=64)
+        x_scales = keep.tile([P, PASSES, B * T], U8, name="x_scales", align_bytes=64)
+        tb, grp, codes, scales, perm = {}, {}, {}, {}, {}
+
+        def prep(key, eng):
+            perm[key] = work.tile([P, PASSES, 2, P], F32, name="perm", tag="perm", bufs=4)
+            src = raw[key][:].bitcast(F32).rearrange("p (g c u) -> p g u c", g=PASSES, u=2)
+            if eng == "dve":
+                nc.vector.tensor_copy(out=perm[key][:], in_=src)
+            else:
+                nc.scalar.copy(out=perm[key][:], in_=src)
+
+        def tr_in(key):
+            tb[key] = bank([P, PASSES, 2, P])
+            for g in range(PASSES):
+                for u in range(2):
+                    if key in perm:
+                        w = perm[key][:, g, u, :]
+                    else:
+                        w = raw[key][:].bitcast(F32)[:, 256 * g + u : 256 * (g + 1) : 2]
+                    nc.tensor.transpose(tb[key][:, g, u, :], w, ident[:])
+
+        def cp_in(key, dve=False):
+            grp[key] = work.tile([P, PASSES, P * 4], BF16, name="grp", tag="grp", bufs=6, align_bytes=64)
+            dst = grp[key][:].bitcast(F32).rearrange("p g (r u) -> p g r u", u=2)
+            src = tb[key][:].rearrange("p g u r -> p g r u")
+            if dve:
+                nc.vector.tensor_copy(out=dst, in_=src)
+            else:
+                nc.scalar.copy(out=dst, in_=src)
+
+        def quant(key):
+            if key[0] == "x":
+                cols = slice(key[1] * T, (key[1] + 1) * T)
+                for g in range(PASSES):
+                    nc.vector.quantize_mx(out=x_codes[:, g, cols].bitcast(E5M2), scales=x_scales[:, g, cols], in_=grp[key][:, g, :])
+            else:
+                codes[key] = keep.tile([P, PASSES * P], U32, name="codes_%s%d" % key, align_bytes=64)
+                scales[key] = keep.tile([P, PASSES * P], U8, name="scales_%s%d" % key, align_bytes=64)
+                nc.vector.quantize_mx(out=codes[key][:].bitcast(E4M3), scales=scales[key][:], in_=grp[key][:].rearrange("p g c -> p (g c)"))
+
+        acc = {}
+
+        def mx(n, j, half):
+            acc[n, j, half] = bank([P, HALF])
+            cols = slice(half * HALF, (half + 1) * HALF)
+            for g in range(PASSES):
+                wc = slice(g * P, (g + 1) * P)
+                nc.tensor.matmul_mx(
+                    out=acc[n, j, half][:],
+                    lhsT=codes[n, j][:, wc].bitcast(E4M3),
+                    lhsT_scale=scales[n, j][:, wc],
+                    rhs=x_codes[:, g, cols].bitcast(E5M2),
+                    rhs_scale=x_scales[:, g, cols],
+                    start=(g == 0),
+                    stop=(g == PASSES - 1),
+                )
+
+        ep, s4, s2, th, wh, wtb, wt, otb = {}, {}, {}, {}, {}, {}, {}, {}
+        sums = keep.tile([P, 2, NCH, T], F32, name="sums")
+        rec = keep.tile([P, NCH, T], F32, name="rec")
+
+        def expk(j, half):
+            if half == 0:
+                ep[j] = work.tile([P, 2, 2, HALF], F32, name="ep", tag="ep")
+            nc.scalar.activation(out=ep[j][:, half, 0, :], in_=acc["k", j, half][:], func=ACT.Exp, bias=bkw[:, j : j + 1])
+
+        def ev(j, half):
+            nc.vector.scalar_tensor_tensor(
+                out=ep[j][:, half, 1, :], in0=acc["v", j, half][:], scalar=bcols[:, 2 * NCH + j : 2 * NCH + j + 1],
+                in1=ep[j][:, half, 0, :], op0=ALU.add, op1=ALU.mult)
+
+        def l1(j):
+            s4[j] = work.tile([P, 2, 2, 2 * T], F32, name="s4", tag="s4")
+            eng = nc.gpsimd if (POOL and j < NCH - 1) else nc.vector
+            eng.tensor_tensor(out=s4[j][:].rearrange("p e a c -> p e (a c)"), in0=ep[j][:, 0], in1=ep[j][:, 1], op=ALU.add)
+
+        def l2(j):
+            s2[j] = work.tile([P, 2, 2, T], F32, name="s2", tag="s2")
+            nc.vector.tensor_tensor(out=s2[j][:].rearrange("p e a c -> p e (a c)"), in0=s4[j][:, :, 0, :], in1=s4[j][:, :, 1, :], op=ALU.add)
+
+        def l3(j):
+            nc.vector.tensor_tensor(out=sums[:, :, j, :], in0=s2[j][:, :, 0, :], in1=s2[j][:, :, 1, :], op=ALU.add)
+
+        def recip(j):
+            nc.vector.reciprocal(out=rec[:, j, :], in_=sums[:, 0, j, :])
+
+        def recip_act(j0, j1):
+            lg = work.tile([P, j1 - j0, T], F32, name="lg", tag="lg", bufs=1)
+            nc.scalar.activation(out=lg[:], in_=sums[:, 0, j0:j1, :], func=ACT.Ln)
+            nc.scalar.activation(out=rec[:, j0:j1, :], in_=lg[:], func=ACT.Exp, scale=-1.0)
+
+        def wmul(j):
+            wh[j] = work.tile([P, T], F32, name="wh", tag="wh", bufs=8)
+            nc.vector.scalar_tensor_tensor(out=wh[j][:], in0=sums[:, 1, j, :], scalar=0.5, in1=rec[:, j, :], op0=ALU.mult, op1=ALU.mult)
+
+        def wtr(j):
+            wtb[j] = bank([P, P])
+            nc.tensor.transpose(wtb[j][:], wh[j][:], ident[:])
+
+        def wcp(j):
+            wt[j] = work.tile([P, P], F32, name="wt", tag="wt")
+            nc.scalar.copy(out=wt[j][:], in_=wtb[j][:])
+
+        def tanhq(j, half):
+            th[j, half] = work.tile([P, HALF], F32, name="th", tag="th", bufs=8)
+            nc.scalar.activation(out=th[j, half][:], in_=acc["q", j, half][:], func=ACT.Tanh, bias=bq_half[:, j : j + 1], scale=0.5)
+
+        def otr(j, half):
+            otb[j, half] = bank([P, 4, P])
+            for i in range(4):
+                nc.tensor.transpose(otb[j, half][:, i, :], th[j, half][:, i * T : (i + 1) * T], ident[:])
+
+        def final(j, half):
+            res = work.tile([P, 4, P], F32, name="res", tag="res", bufs=6)
+            nc.vector.scalar_tensor_tensor(
+                out=res[:], in0=otb[j, half][:], scalar=1.0, in1=wt[j][:].unsqueeze(1).to_broadcast([P, 4, P]),
+                op0=ALU.add, op1=ALU.mult)
+            nc.sync.dma_start(out=out[4 * half : 4 * half + 4, :, j * P : (j + 1) * P].rearrange("b t h -> t b h"), in_=res[:])
+
+        def ok(j):
+            return 0 <= j < NCH
+
+        def pre(keys):
+            for key in keys:
+                if key in PRE_DVE:
+                    prep(key, "dve")
+                elif key in PRE_ACT:
+                    prep(key, "act")
+
+        def kv(j, half):
+            mx("k", j, half)
+            expk(j, half)
+            mx("v", j, half)
+            ev(j, half)
+
+        def qq(j):
+            for half in range(2):
+                mx("q", j, half)
+                tanhq(j, half)
+
+        def feed(keys, lagq):
+            for key in keys:
+                tr_in(key)
+                cp_in(key)
+                lagq.append(key)
+                if len(lagq) > 1:
+                    quant(lagq.pop(0))
+
+        lagq = []
+        feed([("k", 0)] + [("x", b) for b in range(4)], lagq)
+        bias_setup()
+        feed([("v", 0)], lagq)
+        bias_setup2()
+        feed([("x", 4)], lagq)
+        kv(0, 0)
+        feed([("x", 5), ("x", 6), ("x", 7), ("k", 1), ("v", 1)], lagq)
+        quant(lagq.pop(0))
+        kv(0, 1)
+
+        def keys_a(s):
+            ks = [("k", s), ("v", s)] if ok(s) else []
+            if ok(s - LQ):
+                ks.append(("q", s - LQ))
+            return [k for k in ks if k not in tb]
+
+        def do(fn, j, *a):
+            if ok(j):
+                fn(j, *a)
+
+        pre(keys_a(2))
+        if POOL:
+            l1(0)
+        for s in range(1, NCH + LQ + 1):
+            nxt = keys_a(s) + keys_a(s + 1)
+            jo = s - LQ - 1
+            for key in nxt:
+                tr_in(key)
+                cp_in(key)
+            pre(keys_a(s + 2))
+            if ok(jo):
+                wtr(jo)
+                wcp(jo)
+                otr(jo, 0)
+                otr(jo, 1)
+            nq = list(nxt)
+
+            def q1():
+                if nq:
+                    quant(nq.pop(0))
+
+            if POOL:
+                do(recip, s - 2)
+                do(final, jo, 0)
+                do(final, jo, 1)
+                do(wmul, s - 2)
+                do(l2, s - 1)
+                q1()
+                do(l3, s - 1)
+                while nq:
+                    q1()
+                do(kv, s, 0)
+                do(kv, s, 1)
+                do(l1, s)
+            else:
+                q1()
+                do(l1, s - 1)
+                q1()
+                do(l2, s - 1)
+                while nq:
+                    q1()
+                do(l3, s - 1)
+                do(final, jo, 0)
+                do(recip, s - 1)
+                do(final, jo, 1)
+                do(kv, s, 0)
+                do(wmul, s - 1)
+                do(kv, s, 1)
+            do(qq, s - LQ)

@@ -16,16 +16,26 @@ ALU = mybir.AluOpType
 ACT = mybir.ActivationFunctionType
 
 P = 128
-PASSES = 2
-NCH = H // P
-HALF = 512
-LQ = 1
-POOL = False
-LNCH = 6
-PRE_X = 0
-PRE_DVE = ()
-PRE_ACT = ()
-XCOPY_DVE = ()
+PACK = 4
+PASSES = D // (P * PACK)
+CHUNKS = H // P
+LAST = CHUNKS - 1
+HALF_B = B // 2
+HALF = HALF_B * T
+DENOM, NUMER = 0, 1
+
+FIRST_STEP = 2
+PAIRS = dict(
+    [(("k", j), ("v", j)) for j in range(CHUNKS)] + [(("q", 0), ("q", 1)), (("q", LAST - 1), ("q", LAST))]
+)
+
+
+def step_tiles(s):
+    if s > LAST:
+        return []
+    q_from = 0 if s == FIRST_STEP else s - 1
+    q_to = s if s == LAST else s - 1
+    return [(n, s + 1) for n in "kv" if s < LAST] + [("q", j) for j in range(q_from, q_to + 1)]
 
 
 def tile_aftattention_kernel(tc, x, Wq, bq, Wk, bk, Wv, bv, wbias, out):
@@ -42,263 +52,323 @@ def tile_aftattention_kernel(tc, x, Wq, bq, Wk, bk, Wv, bv, wbias, out):
         weights = {"q": Wq, "k": Wk, "v": Wv}
         raw = {}
 
-        def load(key, src):
+        def load(key):
+            name, i = key
             raw[key] = keep.tile([P, D], BF16, name="raw_%s%d" % key)
-            nc.sync.dma_start(out=raw[key][:], in_=src)
+            nc.sync.dma_start(out=raw[key][:], in_=x[i] if name == "x" else weights[name][i * P : (i + 1) * P, :])
 
-        def load_w(n, j):
-            load((n, j), weights[n][j * P : (j + 1) * P, :])
-
-        load_w("k", 0)
-        for b in range(4):
-            load(("x", b), x[b])
-        brows = keep.tile([P, P], BF16, name="brows")
-        nc.vector.memset(brows[:], 0.0)
-        for i, v in enumerate((bq, bk, bv, wbias)):
-            nc.sync.dma_start(out=brows[NCH * i : NCH * (i + 1), :], in_=v.rearrange("(c p) -> c p", p=P))
-        load_w("v", 0)
-        for b in range(4, 8):
-            load(("x", b), x[b])
-        for s in range(1, NCH + LQ):
-            if s < NCH:
-                load_w("k", s)
-                load_w("v", s)
-            if 0 <= s - LQ < NCH:
-                load_w("q", s - LQ)
+        first_half = [("x", b) for b in range(HALF_B)]
+        second_half = [("x", b) for b in range(HALF_B, B)]
+        for key in [("k", 0)] + first_half:
+            load(key)
+        bias_rows = keep.tile([P, P], BF16, name="bias_rows")
+        nc.vector.memset(bias_rows[:], 0.0)
+        for i, vec in enumerate((bq, bk, bv, wbias)):
+            nc.sync.dma_start(out=bias_rows[CHUNKS * i : CHUNKS * (i + 1), :], in_=vec.rearrange("(c p) -> c p", p=P))
+        for key in [("v", 0), ("k", 1), ("v", 1)] + second_half + [("k", FIRST_STEP), ("v", FIRST_STEP)]:
+            load(key)
+        for s in range(FIRST_STEP, CHUNKS):
+            for key in step_tiles(s):
+                load(key)
 
         ident = keep.tile([P, P], F32, name="ident")
         make_identity(nc, ident[:])
         ident_bf = keep.tile([P, P], BF16, name="ident_bf")
         nc.scalar.activation(out=ident_bf[:], in_=ident[:], func=ACT.Copy)
-        bcols = keep.tile([P, 4 * NCH], F32, name="bcols")
-        bq_half = keep.tile([P, NCH], F32, name="bq_half")
-        bkw = keep.tile([P, NCH], F32, name="bkw")
 
-        def bias_setup():
-            bb = bank([P, P], BF16)
-            nc.tensor.transpose(bb[:], brows[:], ident_bf[:])
-            nc.vector.tensor_copy(out=bcols[:], in_=bb[:, : 4 * NCH])
+        bias_cols = keep.tile([P, 4 * CHUNKS], F32, name="bias_cols")
+        half_bq = keep.tile([P, CHUNKS], F32, name="half_bq")
+        exp_bias = keep.tile([P, CHUNKS], F32, name="exp_bias")
 
-        def bias_setup2():
-            nc.vector.tensor_scalar(out=bq_half[:], in0=bcols[:, 0:NCH], scalar1=0.5, scalar2=None, op0=ALU.mult)
-            nc.vector.tensor_tensor(out=bkw[:], in0=bcols[:, NCH : 2 * NCH], in1=bcols[:, 3 * NCH :], op=ALU.add)
+        def transpose_biases():
+            turned = bank([P, P], BF16)
+            nc.tensor.transpose(turned[:], bias_rows[:], ident_bf[:])
+            nc.vector.tensor_copy(out=bias_cols[:], in_=turned[:, : 4 * CHUNKS])
+
+        def combine_biases():
+            nc.vector.tensor_scalar(out=half_bq[:], in0=bias_cols[:, :CHUNKS], scalar1=0.5, scalar2=None, op0=ALU.mult)
+            nc.vector.tensor_tensor(
+                out=exp_bias[:], in0=bias_cols[:, CHUNKS : 2 * CHUNKS], in1=bias_cols[:, 3 * CHUNKS :], op=ALU.add
+            )
 
         x_codes = keep.tile([P, PASSES, B * T], U32, name="x_codes", align_bytes=64)
         x_scales = keep.tile([P, PASSES, B * T], U8, name="x_scales", align_bytes=64)
-        tb, grp, codes, scales, perm = {}, {}, {}, {}, {}
+        sorted_words, staged, staged_pair, w_codes, w_scales = {}, {}, {}, {}, {}
 
-        def prep(key, eng):
-            perm[key] = work.tile([P, PASSES, 2, P], F32, name="perm", tag="perm", bufs=4)
-            src = raw[key][:].bitcast(F32).rearrange("p (g c u) -> p g u c", g=PASSES, u=2)
-            if eng == "dve":
-                nc.vector.tensor_copy(out=perm[key][:], in_=src)
+        def sort_words(key, engine):
+            dst = work.tile([P, PASSES, 2, P], F32, name="sorted", tag="sorted_" + engine, bufs=5)
+            src = raw[key][:].bitcast(F32).rearrange("r (g p u) -> r g u p", g=PASSES, u=2)
+            if engine == "vector":
+                nc.vector.tensor_copy(out=dst[:], in_=src)
             else:
-                nc.scalar.copy(out=perm[key][:], in_=src)
+                nc.scalar.copy(out=dst[:], in_=src)
+            sorted_words[key] = dst
 
-        def tr_in(key):
-            tb[key] = bank([P, PASSES, 2, P])
+        def q_buffer(shape, dtype, name):
+            return work.tile(shape, dtype, name=name, tag="q_buffer", bufs=1, align_bytes=64)
+
+        def stage(key):
+            turned = bank([P, PASSES, 2, P])
             for g in range(PASSES):
                 for u in range(2):
-                    if key in perm:
-                        w = perm[key][:, g, u, :]
+                    if key in sorted_words:
+                        words = sorted_words[key][:, g, u, :]
                     else:
-                        w = raw[key][:].bitcast(F32)[:, 256 * g + u : 256 * (g + 1) : 2]
-                    nc.tensor.transpose(tb[key][:, g, u, :], w, ident[:])
+                        words = raw[key][:].bitcast(F32)[:, 2 * P * g + u : 2 * P * (g + 1) : 2]
+                    nc.tensor.transpose(turned[:, g, u, :], words, ident[:])
+            if key in PAIRS:
+                shape = [P, 2, PASSES, P * PACK]
+                if key[0] == "q":
+                    pair = q_buffer(shape, BF16, "staged_qq")
+                else:
+                    pair = work.tile(shape, BF16, name="staged_kv", align_bytes=64)
+                staged_pair[key] = pair
+                staged[key], staged[PAIRS[key]] = pair[:, 0], pair[:, 1]
+            elif key[0] == "x":
+                staged[key] = work.tile([P, PASSES, P * PACK], BF16, name="staged_x", align_bytes=64)[:]
+            elif key not in staged:
+                staged[key] = q_buffer([P, PASSES, P * PACK], BF16, "staged_q")[:]
+            nc.scalar.copy(
+                out=staged[key].bitcast(F32).rearrange("p g (r u) -> p g r u", u=2),
+                in_=turned[:].rearrange("p g u r -> p g r u"),
+            )
 
-        def cp_in(key, dve=False):
-            grp[key] = work.tile([P, PASSES, P * 4], BF16, name="grp", tag="grp", bufs=6, align_bytes=64)
-            dst = grp[key][:].bitcast(F32).rearrange("p g (r u) -> p g r u", u=2)
-            src = tb[key][:].rearrange("p g u r -> p g r u")
-            if dve:
-                nc.vector.tensor_copy(out=dst, in_=src)
-            else:
-                nc.scalar.copy(out=dst, in_=src)
+        def quantise_weights(keys, src):
+            width = PASSES * P
+            codes = keep.tile([P, len(keys) * width], U32, name="codes_%s%d" % keys[0], align_bytes=64)
+            scales = keep.tile([P, len(keys) * width], U8, name="scales_%s%d" % keys[0], align_bytes=64)
+            nc.vector.quantize_mx(out=codes[:].bitcast(E4M3), scales=scales[:], in_=src)
+            for i, key in enumerate(keys):
+                w_codes[key] = codes[:, i * width : (i + 1) * width]
+                w_scales[key] = scales[:, i * width : (i + 1) * width]
 
-        def quant(key):
+        def quantise(key):
             if key[0] == "x":
-                cols = slice(key[1] * T, (key[1] + 1) * T)
+                tokens = slice(key[1] * T, (key[1] + 1) * T)
                 for g in range(PASSES):
-                    nc.vector.quantize_mx(out=x_codes[:, g, cols].bitcast(E5M2), scales=x_scales[:, g, cols], in_=grp[key][:, g, :])
+                    nc.vector.quantize_mx(
+                        out=x_codes[:, g, tokens].bitcast(E5M2), scales=x_scales[:, g, tokens], in_=staged[key][:, g, :]
+                    )
             else:
-                codes[key] = keep.tile([P, PASSES * P], U32, name="codes_%s%d" % key, align_bytes=64)
-                scales[key] = keep.tile([P, PASSES * P], U8, name="scales_%s%d" % key, align_bytes=64)
-                nc.vector.quantize_mx(out=codes[key][:].bitcast(E4M3), scales=scales[key][:], in_=grp[key][:].rearrange("p g c -> p (g c)"))
+                quantise_weights([key], staged[key].rearrange("p g c -> p (g c)"))
 
-        acc = {}
+        def quantise_pair(key):
+            quantise_weights([key, PAIRS[key]], staged_pair[key][:].rearrange("p n g c -> p (n g c)"))
 
-        def mx(n, j, half):
-            acc[n, j, half] = bank([P, HALF])
-            cols = slice(half * HALF, (half + 1) * HALF)
+        def project(name, j, half):
+            acc = bank([P, HALF])
+            tokens = slice(half * HALF, (half + 1) * HALF)
             for g in range(PASSES):
-                wc = slice(g * P, (g + 1) * P)
+                channels = slice(g * P, (g + 1) * P)
                 nc.tensor.matmul_mx(
-                    out=acc[n, j, half][:],
-                    lhsT=codes[n, j][:, wc].bitcast(E4M3),
-                    lhsT_scale=scales[n, j][:, wc],
-                    rhs=x_codes[:, g, cols].bitcast(E5M2),
-                    rhs_scale=x_scales[:, g, cols],
+                    out=acc[:],
+                    lhsT=w_codes[name, j][:, channels].bitcast(E4M3),
+                    lhsT_scale=w_scales[name, j][:, channels],
+                    rhs=x_codes[:, g, tokens].bitcast(E5M2),
+                    rhs_scale=x_scales[:, g, tokens],
                     start=(g == 0),
                     stop=(g == PASSES - 1),
                 )
+            return acc
 
-        ep, s4, s2, th, wh, wtb, wt, otb = {}, {}, {}, {}, {}, {}, {}, {}
-        sums = keep.tile([P, 2, NCH, T], F32, name="sums")
-        rec = keep.tile([P, NCH, T], F32, name="rec")
+        terms, partial, parts, sums, inverse, half_weighted = {}, {}, {}, {}, {}, {}
 
-        def expk(j, half):
+        def numerators(j, half):
             if half == 0:
-                ep[j] = work.tile([P, 2, 2, HALF], F32, name="ep", tag="ep")
-            nc.scalar.activation(out=ep[j][:, half, 0, :], in_=acc["k", j, half][:], func=ACT.Exp, bias=bkw[:, j : j + 1])
+                terms[j] = work.tile([P, 2, 2, HALF], F32, name="terms")
+            nc.scalar.activation(
+                out=terms[j][:, half, DENOM, :], in_=project("k", j, half)[:], func=ACT.Exp, bias=exp_bias[:, j : j + 1]
+            )
 
-        def ev(j, half):
+        def weigh_values(j, half, v_bank):
             nc.vector.scalar_tensor_tensor(
-                out=ep[j][:, half, 1, :], in0=acc["v", j, half][:], scalar=bcols[:, 2 * NCH + j : 2 * NCH + j + 1],
-                in1=ep[j][:, half, 0, :], op0=ALU.add, op1=ALU.mult)
+                out=terms[j][:, half, NUMER, :],
+                in0=v_bank[:],
+                scalar=bias_cols[:, 2 * CHUNKS + j : 2 * CHUNKS + j + 1],
+                in1=terms[j][:, half, DENOM, :],
+                op0=ALU.add,
+                op1=ALU.mult,
+            )
 
-        def l1(j):
-            s4[j] = work.tile([P, 2, 2, 2 * T], F32, name="s4", tag="s4")
-            eng = nc.gpsimd if (POOL and j < NCH - 1) else nc.vector
-            eng.tensor_tensor(out=s4[j][:].rearrange("p e a c -> p e (a c)"), in0=ep[j][:, 0], in1=ep[j][:, 1], op=ALU.add)
+        def keys_values(j, half):
+            numerators(j, half)
+            weigh_values(j, half, project("v", j, half))
 
-        def l2(j):
-            s2[j] = work.tile([P, 2, 2, T], F32, name="s2", tag="s2")
-            nc.vector.tensor_tensor(out=s2[j][:].rearrange("p e a c -> p e (a c)"), in0=s4[j][:, :, 0, :], in1=s4[j][:, :, 1, :], op=ALU.add)
+        def blocks(ap, n):
+            return [ap[:, i * T : (i + 1) * T] for i in range(n)]
 
-        def l3(j):
-            nc.vector.tensor_tensor(out=sums[:, :, j, :], in0=s2[j][:, :, 0, :], in1=s2[j][:, :, 1, :], op=ALU.add)
+        def first_level(j, engine):
+            partial[j] = work.tile([P, 2, HALF], F32, name="level1", bufs=2)
+            engine.tensor_tensor(out=partial[j][:], in0=terms[j][:, 0], in1=terms[j][:, 1], op=ALU.add)
+            parts[j] = [blocks(partial[j][:, which], HALF_B) for which in (DENOM, NUMER)]
 
-        def recip(j):
-            nc.vector.reciprocal(out=rec[:, j, :], in_=sums[:, 0, j, :])
+        def second_level(j):
+            level2 = q_buffer([P, 2, HALF // 2], F32, "level2")
+            nc.gpsimd.tensor_tensor(
+                out=level2[:], in0=partial[j][:, :, : HALF // 2], in1=partial[j][:, :, HALF // 2 :], op=ALU.add
+            )
+            parts[j] = [blocks(level2[:, which], HALF_B // 2) for which in (DENOM, NUMER)]
 
-        def recip_act(j0, j1):
-            lg = work.tile([P, j1 - j0, T], F32, name="lg", tag="lg", bufs=1)
-            nc.scalar.activation(out=lg[:], in_=sums[:, 0, j0:j1, :], func=ACT.Ln)
-            nc.scalar.activation(out=rec[:, j0:j1, :], in_=lg[:], func=ACT.Exp, scale=-1.0)
+        def first_level_numer_only(j):
+            partial[j] = work.tile([P, HALF], F32, name="level1", bufs=2)
+            nc.gpsimd.tensor_tensor(
+                out=partial[j][:], in0=terms[j][:, 0, NUMER], in1=terms[j][:, 1, NUMER], op=ALU.add
+            )
+            parts[j] = [
+                blocks(terms[j][:, 0, DENOM], HALF_B) + blocks(terms[j][:, 1, DENOM], HALF_B),
+                blocks(partial[j][:], HALF_B),
+            ]
 
-        def wmul(j):
-            wh[j] = work.tile([P, T], F32, name="wh", tag="wh", bufs=8)
-            nc.vector.scalar_tensor_tensor(out=wh[j][:], in0=sums[:, 1, j, :], scalar=0.5, in1=rec[:, j, :], op0=ALU.mult, op1=ALU.mult)
+        def finish_sums(j, wanted=(DENOM, NUMER)):
+            turned = bank([P, len(wanted), P])
+            for place, which in enumerate(wanted):
+                sums[j, which] = turned[:, place, :]
+                for i, block in enumerate(parts[j][which]):
+                    nc.tensor.matmul(
+                        out=sums[j, which],
+                        lhsT=block,
+                        rhs=ident[:],
+                        start=(i == 0),
+                        stop=(i == len(parts[j][which]) - 1),
+                        is_transpose=True,
+                    )
 
-        def wtr(j):
-            wtb[j] = bank([P, P])
-            nc.tensor.transpose(wtb[j][:], wh[j][:], ident[:])
+        def invert(j):
+            inverse[j] = work.tile([P, P], F32, name="inverse")
+            nc.vector.reciprocal(out=inverse[j][:], in_=sums[j, DENOM])
 
-        def wcp(j):
-            wt[j] = work.tile([P, P], F32, name="wt", tag="wt")
-            nc.scalar.copy(out=wt[j][:], in_=wtb[j][:])
-
-        def tanhq(j, half):
-            th[j, half] = work.tile([P, HALF], F32, name="th", tag="th", bufs=8)
-            nc.scalar.activation(out=th[j, half][:], in_=acc["q", j, half][:], func=ACT.Tanh, bias=bq_half[:, j : j + 1], scale=0.5)
-
-        def otr(j, half):
-            otb[j, half] = bank([P, 4, P])
-            for i in range(4):
-                nc.tensor.transpose(otb[j, half][:, i, :], th[j, half][:, i * T : (i + 1) * T], ident[:])
-
-        def final(j, half):
-            res = work.tile([P, 4, P], F32, name="res", tag="res", bufs=6)
+        def divide(j):
+            half_weighted[j] = work.tile([P, P], F32, name="half_weighted", bufs=4)
             nc.vector.scalar_tensor_tensor(
-                out=res[:], in0=otb[j, half][:], scalar=1.0, in1=wt[j][:].unsqueeze(1).to_broadcast([P, 4, P]),
-                op0=ALU.add, op1=ALU.mult)
-            nc.sync.dma_start(out=out[4 * half : 4 * half + 4, :, j * P : (j + 1) * P].rearrange("b t h -> t b h"), in_=res[:])
+                out=half_weighted[j][:], in0=sums[j, NUMER], scalar=0.5, in1=inverse[j][:], op0=ALU.mult, op1=ALU.mult
+            )
 
-        def ok(j):
-            return 0 <= j < NCH
+        tanh_q, tanh_turned = {}, {}
 
-        def pre(keys):
-            for key in keys:
-                if key in PRE_DVE:
-                    prep(key, "dve")
-                elif key in PRE_ACT:
-                    prep(key, "act")
-
-        def kv(j, half):
-            mx("k", j, half)
-            expk(j, half)
-            mx("v", j, half)
-            ev(j, half)
-
-        def qq(j):
+        def queries(j):
             for half in range(2):
-                mx("q", j, half)
-                tanhq(j, half)
+                acc = project("q", j, half)
+                tanh_q[j, half] = work.tile([P, HALF], F32, name="tanh_q", bufs=8)
+                nc.scalar.activation(
+                    out=tanh_q[j, half][:], in_=acc[:], func=ACT.Tanh, bias=half_bq[:, j : j + 1], scale=0.5
+                )
 
-        def feed(keys, lagq):
+        def turn_gates(j, half):
+            tanh_turned[j, half] = bank([P, HALF_B, P])
+            for i, block in enumerate(blocks(tanh_q[j, half][:], HALF_B)):
+                nc.tensor.transpose(tanh_turned[j, half][:, i, :], block, ident[:])
+
+        def emit(j, half):
+            result = work.tile([P, HALF_B, P], F32, name="result", bufs=6)
+            nc.vector.scalar_tensor_tensor(
+                out=result[:],
+                in0=tanh_turned[j, half][:],
+                scalar=1.0,
+                in1=half_weighted[j][:].unsqueeze(1).to_broadcast([P, HALF_B, P]),
+                op0=ALU.add,
+                op1=ALU.mult,
+            )
+            rows = out[half * HALF_B : (half + 1) * HALF_B, :, j * P : (j + 1) * P]
+            nc.sync.dma_start(out=rows.rearrange("b t h -> t b h"), in_=result[:])
+
+        waiting = []
+
+        def feed(keys):
             for key in keys:
-                tr_in(key)
-                cp_in(key)
-                lagq.append(key)
-                if len(lagq) > 1:
-                    quant(lagq.pop(0))
+                stage(key)
+                waiting.append(key)
+                if len(waiting) > 1:
+                    quantise(waiting.pop(0))
 
-        lagq = []
-        feed([("k", 0)] + [("x", b) for b in range(4)], lagq)
-        bias_setup()
-        feed([("v", 0)], lagq)
-        bias_setup2()
-        feed([("x", 4)], lagq)
-        kv(0, 0)
-        feed([("x", 5), ("x", 6), ("x", 7), ("k", 1), ("v", 1)], lagq)
-        quant(lagq.pop(0))
-        kv(0, 1)
+        feed([("k", 0)] + first_half)
+        transpose_biases()
+        feed([("v", 0)])
+        combine_biases()
+        feed([("k", 1)])
+        for key in [("v", 1), second_half[0]]:
+            sort_words(key, "vector")
+        quantise(waiting.pop(0))
+        for key in second_half[1:]:
+            sort_words(key, "vector")
+        numerators(0, 0)
+        v_bank = project("v", 0, 0)
+        feed([("v", 1), second_half[0]])
+        weigh_values(0, 0, v_bank)
+        feed(second_half[1:])
+        quantise(waiting.pop(0))
+        keys_values(1, 0)
+        stage(("k", FIRST_STEP))
+        stage(("v", FIRST_STEP))
+        for key in step_tiles(FIRST_STEP)[:2]:
+            sort_words(key, "vector")
+        keys_values(0, 1)
+        quantise_pair(("k", FIRST_STEP))
+        first_level(0, nc.vector)
+        keys_values(1, 1)
+        first_level(1, nc.vector)
 
-        def keys_a(s):
-            ks = [("k", s), ("v", s)] if ok(s) else []
-            if ok(s - LQ):
-                ks.append(("q", s - LQ))
-            return [k for k in ks if k not in tb]
-
-        def do(fn, j, *a):
-            if ok(j):
-                fn(j, *a)
-
-        pre(keys_a(2))
-        if POOL:
-            l1(0)
-        for s in range(1, NCH + LQ + 1):
-            nxt = keys_a(s) + keys_a(s + 1)
-            jo = s - LQ - 1
-            for key in nxt:
-                tr_in(key)
-                cp_in(key)
-            pre(keys_a(s + 2))
-            if ok(jo):
-                wtr(jo)
-                wcp(jo)
-                otr(jo, 0)
-                otr(jo, 1)
-            nq = list(nxt)
-
-            def q1():
-                if nq:
-                    quant(nq.pop(0))
-
-            if POOL:
-                do(recip, s - 2)
-                do(final, jo, 0)
-                do(final, jo, 1)
-                do(wmul, s - 2)
-                do(l2, s - 1)
-                q1()
-                do(l3, s - 1)
-                while nq:
-                    q1()
-                do(kv, s, 0)
-                do(kv, s, 1)
-                do(l1, s)
+        for s in range(FIRST_STEP, CHUNKS):
+            q_tiles = [key for key in step_tiles(s) if key[0] == "q"]
+            upcoming = step_tiles(s + 1)
+            for key in step_tiles(s):
+                stage(key)
+            for key in upcoming[:1]:
+                sort_words(key, "scalar")
+            if s > FIRST_STEP:
+                turn_gates(s - 3, 0)
+                turn_gates(s - 3, 1)
+            finish_sums(s - 2)
+            if s > FIRST_STEP:
+                emit(s - 3, 0)
+                emit(s - 3, 1)
+            if s == FIRST_STEP:
+                quantise_pair(q_tiles[0])
+                invert(s - 2)
+                quantise_pair(("k", s + 1))
+                divide(s - 2)
+            elif s < LAST:
+                invert(s - 2)
+                quantise_pair(("k", s + 1))
+                divide(s - 2)
+                quantise(q_tiles[0])
             else:
-                q1()
-                do(l1, s - 1)
-                q1()
-                do(l2, s - 1)
-                while nq:
-                    q1()
-                do(l3, s - 1)
-                do(final, jo, 0)
-                do(recip, s - 1)
-                do(final, jo, 1)
-                do(kv, s, 0)
-                do(wmul, s - 1)
-                do(kv, s, 1)
-            do(qq, s - LQ)
+                invert(s - 2)
+                quantise_pair(q_tiles[0])
+                divide(s - 2)
+            for key in upcoming[2:]:
+                sort_words(key, "vector")
+            if len(q_tiles) == 1:
+                second_level(s - 1)
+            if s == LAST:
+                queries(s - 2)
+            keys_values(s, 0)
+            for key in upcoming[1:2]:
+                sort_words(key, "scalar")
+            keys_values(s, 1)
+            if s < LAST:
+                first_level(s, nc.gpsimd)
+                queries(s - 2)
+            else:
+                first_level_numer_only(s)
+
+        turn_gates(LAST - 2, 0)
+        finish_sums(LAST - 1)
+        turn_gates(LAST - 2, 1)
+        finish_sums(LAST, (DENOM,))
+        emit(LAST - 2, 0)
+        invert(LAST - 1)
+        emit(LAST - 2, 1)
+        divide(LAST - 1)
+        invert(LAST)
+        queries(LAST - 1)
+        finish_sums(LAST, (NUMER,))
+        turn_gates(LAST - 1, 0)
+        turn_gates(LAST - 1, 1)
+        queries(LAST)
+        turn_gates(LAST, 0)
+        turn_gates(LAST, 1)
+        emit(LAST - 1, 0)
+        divide(LAST)
+        emit(LAST - 1, 1)
+        emit(LAST, 0)
+        emit(LAST, 1)

@@ -25,6 +25,7 @@ HALF = HALF_B * T
 DENOM, NUMER = 0, 1
 
 FIRST_STEP = 2
+WARM_AT_START = 3
 PAIRS = dict(
     [(("k", j), ("v", j)) for j in range(CHUNKS)] + [(("q", 0), ("q", 1)), (("q", LAST - 1), ("q", LAST))]
 )
@@ -280,7 +281,18 @@ def tile_aftattention_kernel(tc, x, Wq, bq, Wk, bk, Wv, bv, wbias, out):
                 if len(waiting) > 1:
                     quantise(waiting.pop(0))
 
-        feed([("k", 0)] + first_half)
+        zeros = keep.tile([P, HALF], BF16, name="zeros")
+        nc.vector.memset(zeros[:].bitcast(U32), 0)
+
+        def warm_up():
+            nc.tensor.matmul(out=bank([P, HALF])[:], lhsT=zeros[:, :P], rhs=zeros[:], start=True, stop=True)
+
+        for i in range(WARM_AT_START):
+            warm_up()
+        for i, key in enumerate([("k", 0)] + first_half):
+            feed([key])
+            if i % 2 == 1:
+                warm_up()
         transpose_biases()
         feed([("v", 0)])
         combine_biases()

from contextlib import ExitStack

import concourse.mybir as mybir
from concourse.masks import make_identity

B, T, D, H = 8, 128, 1024, 1024
FLOPS = 3 * 2 * B * T * D * H

F32 = mybir.dt.float32
BF16 = mybir.dt.bfloat16
U32 = mybir.dt.uint32
U8 = mybir.dt.uint8
E4M3 = mybir.dt.float8_e4m3fn_x4
E5M2 = mybir.dt.float8_e5m2_x4
ALU = mybir.AluOpType
ACT = mybir.ActivationFunctionType

P = 128
PACK = 4
PASSES = D // (P * PACK)
CHUNKS = H // P
LAST = CHUNKS - 1
HALF_B = B // 2
HALF = HALF_B * T
DENOM, NUMER = 0, 1

FIRST_STEP = 2
WARM_AT_START = 3
PAIRS = dict(
    [(("k", j), ("v", j)) for j in range(CHUNKS)] + [(("q", 0), ("q", 1)), (("q", LAST - 1), ("q", LAST))]
)


def step_tiles(s):
    if s > LAST:
        return []
    q_from = 0 if s == FIRST_STEP else s - 1
    q_to = s if s == LAST else s - 1
    return [(n, s + 1) for n in "kv" if s < LAST] + [("q", j) for j in range(q_from, q_to + 1)]


def tile_aftattention_kernel(tc, x, Wq, bq, Wk, bk, Wv, bv, wbias, out):
    nc = tc.nc
    with ExitStack() as ctx:
        keep = ctx.enter_context(tc.tile_pool(name="keep", bufs=1))
        work = ctx.enter_context(tc.tile_pool(name="work", bufs=3))
        psum = ctx.enter_context(tc.psum_pool(name="psum", bufs=8))
        ctx.enter_context(tc.manual_schedule())

        def bank(shape, dtype=F32):
            return psum.tile(shape, dtype, name="bank", tag="bank")

        weights = {"q": Wq, "k": Wk, "v": Wv}
        raw = {}

        def load(key):
            name, i = key
            raw[key] = keep.tile([P, D], BF16, name="raw_%s%d" % key)
            nc.sync.dma_start(out=raw[key][:], in_=x[i] if name == "x" else weights[name][i * P : (i + 1) * P, :])

        first_half = [("x", b) for b in range(HALF_B)]
        second_half = [("x", b) for b in range(HALF_B, B)]
        for key in [("k", 0)] + first_half:
            load(key)
        bias_rows = keep.tile([P, P], BF16, name="bias_rows")
        nc.vector.memset(bias_rows[:], 0.0)
        for i, vec in enumerate((bq, bk, bv, wbias)):
            nc.sync.dma_start(out=bias_rows[CHUNKS * i : CHUNKS * (i + 1), :], in_=vec.rearrange("(c p) -> c p", p=P))
        for key in [("v", 0), ("k", 1), ("v", 1)] + second_half + [("k", FIRST_STEP), ("v", FIRST_STEP)]:
            load(key)
        for s in range(FIRST_STEP, CHUNKS):
            for key in step_tiles(s):
                load(key)

        ident = keep.tile([P, P], F32, name="ident")
        make_identity(nc, ident[:])
        ident_bf = keep.tile([P, P], BF16, name="ident_bf")
        nc.scalar.activation(out=ident_bf[:], in_=ident[:], func=ACT.Copy)

        bias_cols = keep.tile([P, 4 * CHUNKS], F32, name="bias_cols")
        half_bq = keep.tile([P, CHUNKS], F32, name="half_bq")
        exp_bias = keep.tile([P, CHUNKS], F32, name="exp_bias")

        def transpose_biases():
            turned = bank([P, P], BF16)
            nc.tensor.transpose(turned[:], bias_rows[:], ident_bf[:])
            nc.vector.tensor_copy(out=bias_cols[:], in_=turned[:, : 4 * CHUNKS])

        def combine_biases():
            nc.vector.tensor_scalar(out=half_bq[:], in0=bias_cols[:, :CHUNKS], scalar1=0.5, scalar2=None, op0=ALU.mult)
            nc.vector.tensor_tensor(
                out=exp_bias[:], in0=bias_cols[:, CHUNKS : 2 * CHUNKS], in1=bias_cols[:, 3 * CHUNKS :], op=ALU.add
            )

        x_codes = keep.tile([P, PASSES, B * T], U32, name="x_codes", align_bytes=64)
        x_scales = keep.tile([P, PASSES, B * T], U8, name="x_scales", align_bytes=64)
        sorted_words, staged, staged_pair, w_codes, w_scales = {}, {}, {}, {}, {}

        def sort_words(key, engine):
            dst = work.tile([P, PASSES, 2, P], F32, name="sorted", tag="sorted_" + engine, bufs=5)
            src = raw[key][:].bitcast(F32).rearrange("r (g p u) -> r g u p", g=PASSES, u=2)
            if engine == "vector":
                nc.vector.tensor_copy(out=dst[:], in_=src)
            else:
                nc.scalar.copy(out=dst[:], in_=src)
            sorted_words[key] = dst

        def q_buffer(shape, dtype, name):
            return work.tile(shape, dtype, name=name, tag="q_buffer", bufs=1, align_bytes=64)

        def stage(key):
            turned = bank([P, PASSES, 2, P])
            for g in range(PASSES):
                for u in range(2):
                    if key in sorted_words:
                        words = sorted_words[key][:, g, u, :]
                    else:
                        words = raw[key][:].bitcast(F32)[:, 2 * P * g + u : 2 * P * (g + 1) : 2]
                    nc.tensor.transpose(turned[:, g, u, :], words, ident[:])
            if key in PAIRS:
                shape = [P, 2, PASSES, P * PACK]
                if key[0] == "q":
                    pair = q_buffer(shape, BF16, "staged_qq")
                else:
                    pair = work.tile(shape, BF16, name="staged_kv", align_bytes=64)
                staged_pair[key] = pair
                staged[key], staged[PAIRS[key]] = pair[:, 0], pair[:, 1]
            elif key[0] == "x":
                staged[key] = work.tile([P, PASSES, P * PACK], BF16, name="staged_x", align_bytes=64)[:]
            elif key not in staged:
                staged[key] = q_buffer([P, PASSES, P * PACK], BF16, "staged_q")[:]
            nc.scalar.copy(
                out=staged[key].bitcast(F32).rearrange("p g (r u) -> p g r u", u=2),
                in_=turned[:].rearrange("p g u r -> p g r u"),
            )

        def quantise_weights(keys, src):
            width = PASSES * P
            codes = keep.tile([P, len(keys) * width], U32, name="codes_%s%d" % keys[0], align_bytes=64)
            scales = keep.tile([P, len(keys) * width], U8, name="scales_%s%d" % keys[0], align_bytes=64)
            nc.vector.quantize_mx(out=codes[:].bitcast(E4M3), scales=scales[:], in_=src)
            for i, key in enumerate(keys):
                w_codes[key] = codes[:, i * width : (i + 1) * width]
                w_scales[key] = scales[:, i * width : (i + 1) * width]

        def quantise(key):
            if key[0] == "x":
                tokens = slice(key[1] * T, (key[1] + 1) * T)
                for g in range(PASSES):
                    nc.vector.quantize_mx(
                        out=x_codes[:, g, tokens].bitcast(E5M2), scales=x_scales[:, g, tokens], in_=staged[key][:, g, :]
                    )
            else:
                quantise_weights([key], staged[key].rearrange("p g c -> p (g c)"))

        def quantise_pair(key):
            quantise_weights([key, PAIRS[key]], staged_pair[key][:].rearrange("p n g c -> p (n g c)"))

        def project(name, j, half):
            acc = bank([P, HALF])
            tokens = slice(half * HALF, (half + 1) * HALF)
            for g in range(PASSES):
                channels = slice(g * P, (g + 1) * P)
                nc.tensor.matmul_mx(
                    out=acc[:],
                    lhsT=w_codes[name, j][:, channels].bitcast(E4M3),
                    lhsT_scale=w_scales[name, j][:, channels],
                    rhs=x_codes[:, g, tokens].bitcast(E5M2),
                    rhs_scale=x_scales[:, g, tokens],
                    start=(g == 0),
                    stop=(g == PASSES - 1),
                )
            return acc

        terms, partial, parts, sums, inverse, half_weighted = {}, {}, {}, {}, {}, {}

        def numerators(j, half):
            if half == 0:
                terms[j] = work.tile([P, 2, 2, HALF], F32, name="terms")
            nc.scalar.activation(
                out=terms[j][:, half, DENOM, :], in_=project("k", j, half)[:], func=ACT.Exp, bias=exp_bias[:, j : j + 1]
            )

        def weigh_values(j, half, v_bank):
            nc.vector.scalar_tensor_tensor(
                out=terms[j][:, half, NUMER, :],
                in0=v_bank[:],
                scalar=bias_cols[:, 2 * CHUNKS + j : 2 * CHUNKS + j + 1],
                in1=terms[j][:, half, DENOM, :],
                op0=ALU.add,
                op1=ALU.mult,
            )

        def keys_values(j, half):
            numerators(j, half)
            weigh_values(j, half, project("v", j, half))

        def blocks(ap, n):
            return [ap[:, i * T : (i + 1) * T] for i in range(n)]

        def first_level(j, engine):
            partial[j] = work.tile([P, 2, HALF], F32, name="level1", bufs=2)
            engine.tensor_tensor(out=partial[j][:], in0=terms[j][:, 0], in1=terms[j][:, 1], op=ALU.add)
            parts[j] = [blocks(partial[j][:, which], HALF_B) for which in (DENOM, NUMER)]

        def second_level(j):
            level2 = q_buffer([P, 2, HALF // 2], F32, "level2")
            nc.gpsimd.tensor_tensor(
                out=level2[:], in0=partial[j][:, :, : HALF // 2], in1=partial[j][:, :, HALF // 2 :], op=ALU.add
            )
            parts[j] = [blocks(level2[:, which], HALF_B // 2) for which in (DENOM, NUMER)]

        def first_level_numer_only(j):
            partial[j] = work.tile([P, HALF], F32, name="level1", bufs=2)
            nc.gpsimd.tensor_tensor(
                out=partial[j][:], in0=terms[j][:, 0, NUMER], in1=terms[j][:, 1, NUMER], op=ALU.add
            )
            parts[j] = [
                blocks(terms[j][:, 0, DENOM], HALF_B) + blocks(terms[j][:, 1, DENOM], HALF_B),
                blocks(partial[j][:], HALF_B),
            ]

        def finish_sums(j, wanted=(DENOM, NUMER)):
            turned = bank([P, len(wanted), P])
            for place, which in enumerate(wanted):
                sums[j, which] = turned[:, place, :]
                for i, block in enumerate(parts[j][which]):
                    nc.tensor.matmul(
                        out=sums[j, which],
                        lhsT=block,
                        rhs=ident[:],
                        start=(i == 0),
                        stop=(i == len(parts[j][which]) - 1),
                        is_transpose=True,
                    )

        def invert(j):
            inverse[j] = work.tile([P, P], F32, name="inverse")
            nc.vector.reciprocal(out=inverse[j][:], in_=sums[j, DENOM])

        def divide(j):
            half_weighted[j] = work.tile([P, P], F32, name="half_weighted", bufs=4)
            nc.vector.scalar_tensor_tensor(
                out=half_weighted[j][:], in0=sums[j, NUMER], scalar=0.5, in1=inverse[j][:], op0=ALU.mult, op1=ALU.mult
            )

        tanh_q, tanh_turned = {}, {}

        def queries(j):
            for half in range(2):
                acc = project("q", j, half)
                tanh_q[j, half] = work.tile([P, HALF], F32, name="tanh_q", bufs=8)
                nc.scalar.activation(
                    out=tanh_q[j, half][:], in_=acc[:], func=ACT.Tanh, bias=half_bq[:, j : j + 1], scale=0.5
                )

        def turn_gates(j, half):
            tanh_turned[j, half] = bank([P, HALF_B, P])
            for i, block in enumerate(blocks(tanh_q[j, half][:], HALF_B)):
                nc.tensor.transpose(tanh_turned[j, half][:, i, :], block, ident[:])

        def emit(j, half):
            result = work.tile([P, HALF_B, P], F32, name="result", bufs=6)
            nc.vector.scalar_tensor_tensor(
                out=result[:],
                in0=tanh_turned[j, half][:],
                scalar=1.0,
                in1=half_weighted[j][:].unsqueeze(1).to_broadcast([P, HALF_B, P]),
                op0=ALU.add,
                op1=ALU.mult,
            )
            rows = out[half * HALF_B : (half + 1) * HALF_B, :, j * P : (j + 1) * P]
            nc.sync.dma_start(out=rows.rearrange("b t h -> t b h"), in_=result[:])

        waiting = []

        def feed(keys):
            for key in keys:
                stage(key)
                waiting.append(key)
                if len(waiting) > 1:
                    quantise(waiting.pop(0))

        zeros = keep.tile([P, HALF], BF16, name="zeros")
        nc.vector.memset(zeros[:].bitcast(U32), 0)

        def warm_up():
            nc.tensor.matmul(out=bank([P, HALF])[:], lhsT=zeros[:, :P], rhs=zeros[:], start=True, stop=True)

        for i in range(WARM_AT_START):
            warm_up()
        for i, key in enumerate([("k", 0)] + first_half):
            feed([key])
            if i % 2 == 1:
                warm_up()
        transpose_biases()
        feed([("v", 0)])
        combine_biases()
        feed([("k", 1)])
        for key in [("v", 1), second_half[0]]:
            sort_words(key, "vector")
        quantise(waiting.pop(0))
        for key in second_half[1:]:
            sort_words(key, "vector")
        numerators(0, 0)
        v_bank = project("v", 0, 0)
        feed([("v", 1), second_half[0]])
        weigh_values(0, 0, v_bank)
        feed(second_half[1:])
        quantise(waiting.pop(0))
        keys_values(1, 0)
        stage(("k", FIRST_STEP))
        stage(("v", FIRST_STEP))
        for key in step_tiles(FIRST_STEP)[:2]:
            sort_words(key, "vector")
        keys_values(0, 1)
        quantise_pair(("k", FIRST_STEP))
        first_level(0, nc.vector)
        keys_values(1, 1)
        first_level(1, nc.vector)

        for s in range(FIRST_STEP, CHUNKS):
            q_tiles = [key for key in step_tiles(s) if key[0] == "q"]
            upcoming = step_tiles(s + 1)
            for key in step_tiles(s):
                stage(key)
            for key in upcoming[:1]:
                sort_words(key, "scalar")
            if s > FIRST_STEP:
                turn_gates(s - 3, 0)
                turn_gates(s - 3, 1)
            finish_sums(s - 2)
            if s > FIRST_STEP:
                emit(s - 3, 0)
                emit(s - 3, 1)
            if s == FIRST_STEP:
                quantise_pair(q_tiles[0])
                invert(s - 2)
                quantise_pair(("k", s + 1))
                divide(s - 2)
            elif s < LAST:
                invert(s - 2)
                quantise_pair(("k", s + 1))
                divide(s - 2)
                quantise(q_tiles[0])
            else:
                invert(s - 2)
                quantise_pair(q_tiles[0])
                divide(s - 2)
            for key in upcoming[2:]:
                sort_words(key, "vector")
            if len(q_tiles) == 1:
                second_level(s - 1)
            if s == LAST:
                queries(s - 2)
            keys_values(s, 0)
            for key in upcoming[1:2]:
                sort_words(key, "scalar")
            keys_values(s, 1)
            if s < LAST:
                first_level(s, nc.gpsimd)
                queries(s - 2)
            else:
                first_level_numer_only(s)

        turn_gates(LAST - 2, 0)
        finish_sums(LAST - 1)
        turn_gates(LAST - 2, 1)
        finish_sums(LAST, (DENOM,))
        emit(LAST - 2, 0)
        invert(LAST - 1)
        emit(LAST - 2, 1)
        divide(LAST - 1)
        invert(LAST)
        queries(LAST - 1)
        finish_sums(LAST, (NUMER,))
        turn_gates(LAST - 1, 0)
        turn_gates(LAST - 1, 1)
        queries(LAST)
        turn_gates(LAST, 0)
        turn_gates(LAST, 1)
        emit(LAST - 1, 0)
        divide(LAST)
        emit(LAST - 1, 1)
        emit(LAST, 0)
        emit(LAST, 1)
